import numpy as np
import ml_dtypes


def mxq(x, axis, fmt="e4m3"):
    dtype, down = {"e4m3": (ml_dtypes.float8_e4m3fn, 7), "e5m2": (ml_dtypes.float8_e5m2, 14)}[fmt]
    v = np.moveaxis(np.asarray(x, np.float32).astype(ml_dtypes.bfloat16).astype(np.float64), axis, -1)
    blocks = v.reshape(v.shape[:-1] + (-1, 32))
    amax = np.abs(blocks).max(-1, keepdims=True)
    byte = np.maximum(np.where(amax > 0, np.frexp(amax)[1] - 1 + 127, 0) - down, 1)
    scale = np.exp2(byte - 127.0)
    codes = (blocks / scale).astype(np.float32).astype(dtype).astype(np.float64)
    return np.moveaxis((codes * scale).reshape(v.shape), -1, axis)


WIDE = False


def mx_kscale(k):
    if not WIDE:
        return np.ones(k)
    levels = np.array([30, -30])
    if k % 512:
        return np.exp2(np.random.permutation(np.resize(levels, k // 32))).repeat(32)
    a = np.empty((k // 512, 16))
    for p in range(k // 512):
        a[p, :8] = np.random.permutation(np.resize(levels, 8))
        for g in range(8):
            far = levels[np.abs(levels - a[p, g]) >= 10]
            a[p, g + 8] = far[np.random.randint(len(far))]
    return np.exp2(a.ravel()).repeat(32)


BF16 = ml_dtypes.bfloat16


def bf(x):
    return np.asarray(x, np.float32).astype(BF16)


def f64(x):
    return np.asarray(x).astype(np.float64)


G, GI, GO, B = 32, 32, 32, 4096
K = G * GI
N = G * GO


def block_gain():
    gain = np.ones((N, K))
    for g in range(G):
        gain[g * GO:(g + 1) * GO, g * GI:(g + 1) * GI] = 0.5
    return gain


def setup_inputs():
    s = mx_kscale(K)
    bound = 1.0 / np.sqrt(K)
    W = np.random.uniform(-bound, bound, (N, K)) * block_gain()
    return {"data": bf(np.random.standard_normal((B, K)) * s),
            "W": bf(W / s[None, :]),
            "b": bf(np.random.standard_normal(N) * 0.3)}


def reference(data, W, b):
    return (mxq(f64(data), 1, "e5m2") @ mxq(f64(W), 1, "e4m3").T) + f64(b)

@@ -1,0 +1,230 @@
+from contextlib import ExitStack
+
+import concourse.mybir as mybir
+from concourse.masks import make_identity
+
+B, K, N = 4096, 1024, 1024
+FLOPS = 2 * B * K * N
+
+F32 = mybir.dt.float32
+BF16 = mybir.dt.bfloat16
+U32 = mybir.dt.uint32
+U8 = mybir.dt.uint8
+E4M3X4 = mybir.dt.float8_e4m3fn_x4
+E5M2X4 = mybir.dt.float8_e5m2_x4
+ADD = mybir.AluOpType.add
+
+P = 128
+PASSES = K // 512
+N_TILE = 512
+HALVES = N // N_TILE
+GROUP = 4
+GROUPS = B // (P * GROUP)
+T_BANKS = 4
+M_BANKS = 4
+OUT_BUFS = 9
+
+
+def tile_groupfc_kernel(tc, data, W, b, out):
+    nc = tc.nc
+
+    with ExitStack() as ctx:
+        keep = ctx.enter_context(tc.tile_pool(name="keep", bufs=1))
+        stage = ctx.enter_context(tc.tile_pool(name="stage", bufs=1))
+        psum = ctx.enter_context(tc.psum_pool(name="psum", bufs=1))
+        ctx.enter_context(tc.manual_schedule())
+
+        ident = keep.tile([P, P], F32, name="ident")
+        make_identity(nc, ident[:])
+        bias_row = keep.tile([P, N], BF16, name="bias_row")
+        ones = keep.tile([P, P], BF16, name="ones")
+        nc.vector.memset(bias_row[:].bitcast(U32), 0)
+        nc.vector.memset(ones[:], 1.0)
+        nc.scalar.dma_start(out=bias_row[0:1, :], in_=b.rearrange("(o n) -> o n", o=1))
+
+        w_raw = {}
+        x_raw = {}
+        out_rows = {}
+
+        def load_w(first, count):
+            t = keep.tile([P, count, K], BF16, name="w_raw%d" % first)
+            nc.sync.dma_start(
+                out=t[:], in_=W[first * P:(first + count) * P, :].rearrange("(j p) k -> p j k", p=P))
+            for j in range(count):
+                w_raw[first + j] = t[:, j, :]
+
+        def load_x(first, count):
+            rows = slice(first * P, (first + count) * P)
+            t = keep.tile([P, count, K], BF16, name="x_raw%d" % first)
+            nc.sync.dma_start(out=t[:], in_=data[rows, :].rearrange("(p j) k -> p j k", j=count))
+            view = out[rows, :].rearrange("(p j) n -> p j n", j=count)
+            for j in range(count):
+                x_raw[first + j] = t[:, j, :]
+            for j in range(0, count, 2):
+                out_rows[(first + j) // 2] = view[:, j:j + 2, :]
+
+        for r in range(4):
+            load_w(r, 1)
+        load_x(0, 2)
+        load_x(2, 2)
+        load_w(4, 2)
+        load_w(6, 2)
+        for s in range(1, GROUPS):
+            load_x(s * GROUP, GROUP)
+
+        w_codes = keep.tile([P, PASSES, N], U32, name="w_codes", align_bytes=64)
+        w_scales = keep.tile([P, PASSES, N], U8, name="w_scales", align_bytes=64)
+        bias = keep.tile([P, N], F32, name="bias")
+
+        t_count = []
+        m_count = []
+
+        def t_bank():
+            t_count.append(0)
+            return psum.tile([P, PASSES, 2, P], F32, name="t_bank%d" % (len(t_count) % T_BANKS))
+
+        def m_bank():
+            m_count.append(0)
+            return psum.tile([P, N_TILE], F32, name="m_bank%d" % (len(m_count) % M_BANKS))
+
+        def copy_out(engine, dst, src):
+            if engine == "scalar":
+                nc.scalar.copy(out=dst, in_=src)
+            else:
+                nc.vector.tensor_copy(out=dst, in_=src)
+
+        def transpose_strided(raw, dst, engine):
+            words = raw.bitcast(F32)
+            bank = t_bank()
+            for g in range(PASSES):
+                for u in range(2):
+                    nc.tensor.transpose(bank[:, g, u, :], words[:, 256 * g + u:256 * (g + 1):2], ident[:])
+            copy_out(engine, dst.bitcast(F32).rearrange("p (g r u) -> p g r u", g=PASSES, u=2),
+                     bank[:].rearrange("p g u r -> p g r u"))
+
+        def transpose_split(split, dst):
+            bank = t_bank()
+            for g in range(PASSES):
+                for u in range(2):
+                    nc.tensor.transpose(bank[:, g, u, :], split[:, g, u, :], ident[:])
+            copy_out("scalar", dst.bitcast(F32).rearrange("p (g r u) -> p g r u", g=PASSES, u=2),
+                     bank[:].rearrange("p g u r -> p g r u"))
+
+        w_grouped = {}
+
+        def w_transpose(r, engine):
+            t = stage.tile([P, K], BF16, name="w_grouped%d" % (r % 4), align_bytes=64)
+            transpose_strided(w_raw[r], t[:], engine)
+            w_grouped[r] = t
+
+        def w_quantize(r):
+            cols = slice(r * P, (r + 1) * P)
+            for g in range(PASSES):
+                nc.vector.quantize_mx(
+                    out=w_codes[:, g, cols].bitcast(E4M3X4), scales=w_scales[:, g, cols],
+                    in_=w_grouped[r][:, 512 * g:512 * (g + 1)])
+
+        split = {}
+        grouped = {}
+        codes = {}
+        scales = {}
+        result = {}
+
+        def x_split(i):
+            t = stage.tile([P, PASSES, 2, P], F32, name="split%d" % (i % 8))
+            nc.scalar.copy(out=t[:], in_=x_raw[i].bitcast(F32).rearrange("p (g q u) -> p g u q", g=PASSES, u=2))
+            split[i] = t
+
+        def x_transpose(i):
+            q = i // 2
+            if i % 2 == 0:
+                grouped[q] = stage.tile([P, 2 * K], BF16, name="grouped%d" % (q % 4), align_bytes=64)
+            dst = grouped[q][:, (i % 2) * K:(i % 2 + 1) * K]
+            if i in split:
+                transpose_split(split[i], dst)
+            else:
+                transpose_strided(x_raw[i], dst, "scalar")
+
+        def x_quantize(first, count):
+            q = first // 2
+            if first % 2 == 0:
+                codes[q] = stage.tile([P, 2 * PASSES * P], U32, name="codes%d" % (q % 4), align_bytes=64)
+                scales[q] = stage.tile([P, 2 * PASSES * P], U8, name="scales%d" % (q % 4), align_bytes=64)
+            j = first % 2
+            cols = slice(j * PASSES * P, (j + count) * PASSES * P)
+            nc.vector.quantize_mx(
+                out=codes[q][:, cols].bitcast(E5M2X4), scales=scales[q][:, cols],
+                in_=grouped[q][:, j * K:(j + count) * K])
+
+        def multiply(i, h):
+            q, j = i // 2, i % 2
+            if q not in result:
+                result[q] = stage.tile([P, 2, N], F32, name="result%d" % (q % OUT_BUFS))
+            n_cols = slice(h * N_TILE, (h + 1) * N_TILE)
+            acc = m_bank()
+            for g in range(PASSES):
+                cols = slice((j * PASSES + g) * P, (j * PASSES + g + 1) * P)
+                nc.tensor.matmul_mx(
+                    out=acc[:], lhsT=codes[q][:, cols].bitcast(E5M2X4), lhsT_scale=scales[q][:, cols],
+                    rhs=w_codes[:, g, n_cols].bitcast(E4M3X4), rhs_scale=w_scales[:, g, n_cols],
+                    start=(g == 0), stop=(g == PASSES - 1))
+            nc.vector.tensor_tensor(out=result[q][:, j, n_cols], in0=acc[:], in1=bias[:, n_cols], op=ADD)
+
+        def store(q):
+            nc.sync.dma_start(out=out_rows[q], in_=result[q][:])
+
+        for r in range(4):
+            w_transpose(r, "scalar" if r % 2 == 0 else "vector")
+            if r > 0:
+                w_quantize(r - 1)
+        for h in range(HALVES):
+            n_cols = slice(h * N_TILE, (h + 1) * N_TILE)
+            spread = m_bank()
+            nc.tensor.matmul(spread[:], ones[:], bias_row[:, n_cols], start=True, stop=True)
+            nc.scalar.copy(out=bias[:, n_cols], in_=spread[:])
+        w_quantize(3)
+        for i in range(GROUP):
+            x_transpose(i)
+            x_quantize(i, 1)
+        multiply(0, 0)
+        multiply(1, 0)
+        w_transpose(4, "scalar")
+        w_transpose(5, "scalar")
+        multiply(2, 0)
+        w_quantize(4)
+        multiply(3, 0)
+        w_quantize(5)
+        w_transpose(6, "scalar")
+        w_transpose(7, "scalar")
+        w_quantize(6)
+        w_quantize(7)
+        for i in range(GROUP, 2 * GROUP):
+            x_transpose(i)
+        for i in range(2 * GROUP, 3 * GROUP):
+            x_split(i)
+        for i in range(GROUP):
+            multiply(i, 1)
+            if i % 2 == 1:
+                x_quantize(GROUP + i - 1, 2)
+                store(i // 2)
+
+        for s in range(1, GROUPS):
+            if s + 1 < GROUPS:
+                for i in range((s + 1) * GROUP, (s + 2) * GROUP):
+                    x_transpose(i)
+            if s + 2 < GROUPS:
+                for i in range((s + 2) * GROUP, (s + 3) * GROUP):
+                    x_split(i)
+            for i in range(s * GROUP, (s + 1) * GROUP):
+                q, j = i // 2, i % 2
+                for h in range(HALVES):
+                    multiply(i, h)
+                    if i == B // P - 1:
+                        n_cols = slice(h * N_TILE, (h + 1) * N_TILE)
+                        nc.sync.dma_start(out=out_rows[q][:, j, n_cols], in_=result[q][:, j, n_cols])
+                if s + 1 < GROUPS:
+                    if j == 1:
+                        x_quantize(i + GROUP - 1, 2)
+                        store(q)
+                elif i < B // P - 1:
+                    nc.sync.dma_start(out=out_rows[q][:, j, :], in_=result[q][:, j, :])

@@ -18,8 +18,11 @@ P = 128
 PASSES = K // 512
 N_TILE = 512
 HALVES = N // N_TILE
-GROUP = 4
-GROUPS = B // (P * GROUP)
+TILES = B // P
+RUN = 4
+HEAD = 6
+LEAD = 2
+FINE = 8
 T_BANKS = 4
 M_BANKS = 4
 OUT_BUFS = 9
@@ -60,17 +63,19 @@ def tile_groupfc_kernel(tc, data, W, b, out):
             view = out[rows, :].rearrange("(p j) n -> p j n", j=count)
             for j in range(count):
                 x_raw[first + j] = t[:, j, :]
-            for j in range(0, count, 2):
-                out_rows[(first + j) // 2] = view[:, j:j + 2, :]
+                out_rows[first + j] = (view, j)
 
+        load_x(0, 1)
         for r in range(4):
             load_w(r, 1)
-        load_x(0, 2)
+        load_x(1, 1)
         load_x(2, 2)
         load_w(4, 2)
         load_w(6, 2)
-        for s in range(1, GROUPS):
-            load_x(s * GROUP, GROUP)
+        load_x(4, 2)
+        runs = [(HEAD, HEAD + 2)] + [(first, first + RUN) for first in range(HEAD + 2, TILES, RUN)]
+        for first, last in runs:
+            load_x(first, last - first)
 
         w_codes = keep.tile([P, PASSES, N], U32, name="w_codes", align_bytes=64)
         w_scales = keep.tile([P, PASSES, N], U8, name="w_scales", align_bytes=64)
@@ -102,20 +107,29 @@ def tile_groupfc_kernel(tc, data, W, b, out):
             copy_out(engine, dst.bitcast(F32).rearrange("p (g r u) -> p g r u", g=PASSES, u=2),
                      bank[:].rearrange("p g u r -> p g r u"))
 
-        def transpose_split(split, dst):
+        def transpose_split(split, dst, engine):
             bank = t_bank()
             for g in range(PASSES):
                 for u in range(2):
                     nc.tensor.transpose(bank[:, g, u, :], split[:, g, u, :], ident[:])
-            copy_out("scalar", dst.bitcast(F32).rearrange("p (g r u) -> p g r u", g=PASSES, u=2),
+            copy_out(engine, dst.bitcast(F32).rearrange("p (g r u) -> p g r u", g=PASSES, u=2),
                      bank[:].rearrange("p g u r -> p g r u"))
 
         w_grouped = {}
+        w_split_tiles = {}
 
         def w_transpose(r, engine):
             t = stage.tile([P, K], BF16, name="w_grouped%d" % (r % 4), align_bytes=64)
-            transpose_strided(w_raw[r], t[:], engine)
+            if r in w_split_tiles:
+                transpose_split(w_split_tiles[r], t[:], engine)
+            else:
+                transpose_strided(w_raw[r], t[:], engine)
             w_grouped[r] = t
+
+        def w_split(r, engine):
+            t = stage.tile([P, PASSES, 2, P], F32, name="w_split%d" % (r % 4))
+            copy_out(engine, t[:], w_raw[r].bitcast(F32).rearrange("p (g q u) -> p g u q", g=PASSES, u=2))
+            w_split_tiles[r] = t
 
         def w_quantize(r):
             cols = slice(r * P, (r + 1) * P)
@@ -130,20 +144,20 @@ def tile_groupfc_kernel(tc, data, W, b, out):
         scales = {}
         result = {}
 
-        def x_split(i):
+        def x_split(i, engine):
             t = stage.tile([P, PASSES, 2, P], F32, name="split%d" % (i % 8))
-            nc.scalar.copy(out=t[:], in_=x_raw[i].bitcast(F32).rearrange("p (g q u) -> p g u q", g=PASSES, u=2))
+            copy_out(engine, t[:], x_raw[i].bitcast(F32).rearrange("p (g q u) -> p g u q", g=PASSES, u=2))
             split[i] = t
 
-        def x_transpose(i):
+        def x_transpose(i, engine):
             q = i // 2
             if i % 2 == 0:
                 grouped[q] = stage.tile([P, 2 * K], BF16, name="grouped%d" % (q % 4), align_bytes=64)
             dst = grouped[q][:, (i % 2) * K:(i % 2 + 1) * K]
             if i in split:
-                transpose_split(split[i], dst)
+                transpose_split(split[i], dst, engine)
             else:
-                transpose_strided(x_raw[i], dst, "scalar")
+                transpose_strided(x_raw[i], dst, engine)
 
         def x_quantize(first, count):
             q = first // 2
@@ -170,61 +184,87 @@ def tile_groupfc_kernel(tc, data, W, b, out):
                     start=(g == 0), stop=(g == PASSES - 1))
             nc.vector.tensor_tensor(out=result[q][:, j, n_cols], in0=acc[:], in1=bias[:, n_cols], op=ADD)
 
-        def store(q):
-            nc.sync.dma_start(out=out_rows[q], in_=result[q][:])
+        def store(i, count, n_cols):
+            view, j = out_rows[i]
+            nc.sync.dma_start(out=view[:, j:j + count, n_cols], in_=result[i // 2][:, i % 2:i % 2 + count, n_cols])
 
-        for r in range(4):
-            w_transpose(r, "scalar" if r % 2 == 0 else "vector")
-            if r > 0:
-                w_quantize(r - 1)
-        for h in range(HALVES):
+        def spread_bias(h, engine):
             n_cols = slice(h * N_TILE, (h + 1) * N_TILE)
             spread = m_bank()
             nc.tensor.matmul(spread[:], ones[:], bias_row[:, n_cols], start=True, stop=True)
-            nc.scalar.copy(out=bias[:, n_cols], in_=spread[:])
+            copy_out(engine, bias[:, n_cols], spread[:])
+
+        def finish(i):
+            if i == TILES - 1:
+                store(i, 1, slice(N_TILE, N))
+            elif i < 2 or i >= TILES - FINE:
+                store(i, 1, slice(0, N))
+            elif i % 2 == 1:
+                store(i - 1, 2, slice(0, N))
+
+        x_transpose(0, "scalar")
+        w_transpose(0, "scalar")
+        x_quantize(0, 1)
+        w_transpose(1, "scalar")
+        w_quantize(0)
+        w_transpose(2, "scalar")
+        w_quantize(1)
+        w_transpose(3, "vector")
+        w_quantize(2)
+        x_transpose(1, "scalar")
         w_quantize(3)
-        for i in range(GROUP):
-            x_transpose(i)
-            x_quantize(i, 1)
+        spread_bias(0, "scalar")
+        x_quantize(1, 1)
+        spread_bias(1, "scalar")
+        x_split(2, "vector")
+        x_split(3, "vector")
+        w_split(4, "scalar")
+        w_split(5, "scalar")
         multiply(0, 0)
         multiply(1, 0)
+        w_split(6, "vector")
+        w_split(7, "vector")
+        x_transpose(2, "scalar")
+        x_transpose(3, "scalar")
+        x_quantize(2, 1)
+        x_quantize(3, 1)
         w_transpose(4, "scalar")
-        w_transpose(5, "scalar")
-        multiply(2, 0)
-        w_quantize(4)
-        multiply(3, 0)
-        w_quantize(5)
+        w_transpose(5, "vector")
         w_transpose(6, "scalar")
         w_transpose(7, "scalar")
+        w_quantize(4)
+        w_quantize(5)
         w_quantize(6)
+        multiply(2, 0)
         w_quantize(7)
-        for i in range(GROUP, 2 * GROUP):
-            x_transpose(i)
-        for i in range(2 * GROUP, 3 * GROUP):
-            x_split(i)
-        for i in range(GROUP):
-            multiply(i, 1)
-            if i % 2 == 1:
-                x_quantize(GROUP + i - 1, 2)
-                store(i // 2)
+        multiply(3, 0)
+        x_transpose(4, "scalar")
+        x_transpose(5, "scalar")
+        x_split(6, "scalar")
+        x_split(7, "scalar")
+        todo = [(i, 1) for i in range(4)] + [(i, h) for i in range(4, TILES) for h in range(HALVES)]
 
-        for s in range(1, GROUPS):
-            if s + 1 < GROUPS:
-                for i in range((s + 1) * GROUP, (s + 2) * GROUP):
-                    x_transpose(i)
-            if s + 2 < GROUPS:
-                for i in range((s + 2) * GROUP, (s + 3) * GROUP):
-                    x_split(i)
-            for i in range(s * GROUP, (s + 1) * GROUP):
-                q, j = i // 2, i % 2
-                for h in range(HALVES):
-                    multiply(i, h)
-                    if i == B // P - 1:
-                        n_cols = slice(h * N_TILE, (h + 1) * N_TILE)
-                        nc.sync.dma_start(out=out_rows[q][:, j, n_cols], in_=result[q][:, j, n_cols])
-                if s + 1 < GROUPS:
-                    if j == 1:
-                        x_quantize(i + GROUP - 1, 2)
-                        store(q)
-                elif i < B // P - 1:
-                    nc.sync.dma_start(out=out_rows[q][:, j, :], in_=result[q][:, j, :])
+        def advance(count):
+            for i, h in todo[:count]:
+                multiply(i, h)
+                if i == TILES - 1 and h == 0:
+                    store(i, 1, slice(0, N_TILE))
+                if h == 1:
+                    finish(i)
+            for step in range(count):
+                todo.pop(0)
+
+        advance(2)
+        x_quantize(4, 2)
+        advance(2)
+
+        for first, last in runs:
+            for i in range(first, last):
+                x_transpose(i, "scalar")
+            x_quantize(first, 2)
+            for i in range(last, min(last + RUN, TILES)):
+                x_split(i, "scalar")
+            for pair in range(first + 2, last, 2):
+                advance(4)
+                x_quantize(pair, 2)
+            advance(4 if last < TILES else len(todo))

@@ -21,11 +21,13 @@ HALVES = N // N_TILE
 TILES = B // P
 RUN = 4
 HEAD = 6
-LEAD = 2
-FINE = 8
+BLOCK = 8
+QUAD = 4
+PAIRS_FROM = 20
+SINGLES_FROM = 26
 T_BANKS = 4
 M_BANKS = 4
-OUT_BUFS = 9
+OUT_BUFS = 5
 
 
 def tile_groupfc_kernel(tc, data, W, b, out):
@@ -47,7 +49,8 @@ def tile_groupfc_kernel(tc, data, W, b, out):
 
         w_raw = {}
         x_raw = {}
-        out_rows = {}
+        data_rows = data.rearrange("(a p j) k -> a p j k", p=P, j=BLOCK)
+        out_rows = out.rearrange("(a p j) n -> a p j n", p=P, j=BLOCK)
 
         def load_w(first, count):
             t = keep.tile([P, count, K], BF16, name="w_raw%d" % first)
@@ -57,13 +60,11 @@ def tile_groupfc_kernel(tc, data, W, b, out):
                 w_raw[first + j] = t[:, j, :]
 
         def load_x(first, count):
-            rows = slice(first * P, (first + count) * P)
+            block, j0 = divmod(first, BLOCK)
             t = keep.tile([P, count, K], BF16, name="x_raw%d" % first)
-            nc.sync.dma_start(out=t[:], in_=data[rows, :].rearrange("(p j) k -> p j k", j=count))
-            view = out[rows, :].rearrange("(p j) n -> p j n", j=count)
+            nc.sync.dma_start(out=t[:], in_=data_rows[block][:, j0:j0 + count, :])
             for j in range(count):
                 x_raw[first + j] = t[:, j, :]
-                out_rows[first + j] = (view, j)
 
         load_x(0, 1)
         for r in range(4):
@@ -74,8 +75,11 @@ def tile_groupfc_kernel(tc, data, W, b, out):
         load_w(6, 2)
         load_x(4, 2)
         runs = [(HEAD, HEAD + 2)] + [(first, first + RUN) for first in range(HEAD + 2, TILES, RUN)]
-        for first, last in runs:
-            load_x(first, last - first)
+        load_x(6, 2)
+        load_x(8, 4)
+        load_x(12, 4)
+        load_x(16, 8)
+        load_x(24, 8)
 
         w_codes = keep.tile([P, PASSES, N], U32, name="w_codes", align_bytes=64)
         w_scales = keep.tile([P, PASSES, N], U8, name="w_scales", align_bytes=64)
@@ -127,7 +131,7 @@ def tile_groupfc_kernel(tc, data, W, b, out):
             w_grouped[r] = t
 
         def w_split(r, engine):
-            t = stage.tile([P, PASSES, 2, P], F32, name="w_split%d" % (r % 4))
+            t = stage.tile([P, PASSES, 2, P], F32, name="split%d" % r)
             copy_out(engine, t[:], w_raw[r].bitcast(F32).rearrange("p (g q u) -> p g u q", g=PASSES, u=2))
             w_split_tiles[r] = t
 
@@ -172,8 +176,8 @@ def tile_groupfc_kernel(tc, data, W, b, out):
 
         def multiply(i, h):
             q, j = i // 2, i % 2
-            if q not in result:
-                result[q] = stage.tile([P, 2, N], F32, name="result%d" % (q % OUT_BUFS))
+            if i // QUAD not in result:
+                result[i // QUAD] = stage.tile([P, QUAD, N], F32, name="result%d" % (i // QUAD % OUT_BUFS))
             n_cols = slice(h * N_TILE, (h + 1) * N_TILE)
             acc = m_bank()
             for g in range(PASSES):
@@ -182,11 +186,12 @@ def tile_groupfc_kernel(tc, data, W, b, out):
                     out=acc[:], lhsT=codes[q][:, cols].bitcast(E5M2X4), lhsT_scale=scales[q][:, cols],
                     rhs=w_codes[:, g, n_cols].bitcast(E4M3X4), rhs_scale=w_scales[:, g, n_cols],
                     start=(g == 0), stop=(g == PASSES - 1))
-            nc.vector.tensor_tensor(out=result[q][:, j, n_cols], in0=acc[:], in1=bias[:, n_cols], op=ADD)
+            nc.vector.tensor_tensor(out=result[i // QUAD][:, i % QUAD, n_cols], in0=acc[:], in1=bias[:, n_cols], op=ADD)
 
         def store(i, count, n_cols):
-            view, j = out_rows[i]
-            nc.sync.dma_start(out=view[:, j:j + count, n_cols], in_=result[i // 2][:, i % 2:i % 2 + count, n_cols])
+            block, j = divmod(i, BLOCK)
+            nc.sync.dma_start(out=out_rows[block][:, j:j + count, n_cols],
+                              in_=result[i // QUAD][:, i % QUAD:i % QUAD + count, n_cols])
 
         def spread_bias(h, engine):
             n_cols = slice(h * N_TILE, (h + 1) * N_TILE)
@@ -197,10 +202,13 @@ def tile_groupfc_kernel(tc, data, W, b, out):
         def finish(i):
             if i == TILES - 1:
                 store(i, 1, slice(N_TILE, N))
-            elif i < 2 or i >= TILES - FINE:
+            elif i >= SINGLES_FROM:
                 store(i, 1, slice(0, N))
-            elif i % 2 == 1:
-                store(i - 1, 2, slice(0, N))
+            elif i >= PAIRS_FROM:
+                if i % 2 == 1:
+                    store(i - 1, 2, slice(0, N))
+            elif i % QUAD == QUAD - 1:
+                store(i - QUAD + 1, QUAD, slice(0, N))
 
         x_transpose(0, "scalar")
         w_transpose(0, "scalar")

@@ -21,12 +21,11 @@ HALVES = N // N_TILE
 TILES = B // P
 RUN = 4
 HEAD = 6
-BLOCK = 8
+BLOCK = 4
 QUAD = 4
-PAIRS_FROM = 20
-SINGLES_FROM = 26
-T_BANKS = 4
-M_BANKS = 4
+PAIRS_FROM = 0
+SINGLES_FROM = 24
+BANKS = 8
 OUT_BUFS = 5
 
 
@@ -76,25 +75,22 @@ def tile_groupfc_kernel(tc, data, W, b, out):
         load_x(4, 2)
         runs = [(HEAD, HEAD + 2)] + [(first, first + RUN) for first in range(HEAD + 2, TILES, RUN)]
         load_x(6, 2)
-        load_x(8, 4)
-        load_x(12, 4)
-        load_x(16, 8)
-        load_x(24, 8)
+        for first in range(8, TILES, RUN):
+            load_x(first, RUN)
 
         w_codes = keep.tile([P, PASSES, N], U32, name="w_codes", align_bytes=64)
         w_scales = keep.tile([P, PASSES, N], U8, name="w_scales", align_bytes=64)
         bias = keep.tile([P, N], F32, name="bias")
 
-        t_count = []
-        m_count = []
+        used = []
 
         def t_bank():
-            t_count.append(0)
-            return psum.tile([P, PASSES, 2, P], F32, name="t_bank%d" % (len(t_count) % T_BANKS))
+            used.append(0)
+            return psum.tile([P, PASSES, 2, P], F32, name="bank%d" % (len(used) % BANKS))
 
         def m_bank():
-            m_count.append(0)
-            return psum.tile([P, N_TILE], F32, name="m_bank%d" % (len(m_count) % M_BANKS))
+            used.append(0)
+            return psum.tile([P, N_TILE], F32, name="bank%d" % (len(used) % BANKS))
 
         def copy_out(engine, dst, src):
             if engine == "scalar":
@@ -229,8 +225,8 @@ def tile_groupfc_kernel(tc, data, W, b, out):
         w_split(4, "scalar")
         w_split(5, "scalar")
         multiply(0, 0)
-        multiply(1, 0)
         w_split(6, "vector")
+        multiply(1, 0)
         w_split(7, "vector")
         x_transpose(2, "scalar")
         x_transpose(3, "scalar")
@@ -246,10 +242,12 @@ def tile_groupfc_kernel(tc, data, W, b, out):
         multiply(2, 0)
         w_quantize(7)
         multiply(3, 0)
-        x_transpose(4, "scalar")
-        x_transpose(5, "scalar")
-        x_split(6, "scalar")
-        x_split(7, "scalar")
+        x_split(8, "scalar")
+        x_split(9, "scalar")
+        for i in range(4, 8):
+            x_transpose(i, "scalar")
+        x_split(10, "vector")
+        x_split(11, "vector")
         todo = [(i, 1) for i in range(4)] + [(i, h) for i in range(4, TILES) for h in range(HALVES)]
 
         def advance(count):
@@ -265,14 +263,24 @@ def tile_groupfc_kernel(tc, data, W, b, out):
         advance(2)
         x_quantize(4, 2)
         advance(2)
+        x_quantize(6, 2)
 
-        for first, last in runs:
+        for first in range(8, TILES - RUN, RUN):
+            last = first + RUN
             for i in range(first, last):
                 x_transpose(i, "scalar")
-            x_quantize(first, 2)
-            for i in range(last, min(last + RUN, TILES)):
+            for i in range(last, last + RUN):
                 x_split(i, "scalar")
-            for pair in range(first + 2, last, 2):
+            for pair in range(first, last, 2):
                 advance(4)
                 x_quantize(pair, 2)
-            advance(4 if last < TILES else len(todo))
+        for i in range(TILES - 4, TILES - 2):
+            x_transpose(i, "scalar")
+        advance(4)
+        x_quantize(TILES - 4, 2)
+        advance(4)
+        for i in range(TILES - 2, TILES):
+            x_transpose(i, "scalar")
+        advance(1)
+        x_quantize(TILES - 2, 2)
+        advance(len(todo))

@@ -15,22 +15,28 @@ E5M2X4 = mybir.dt.float8_e5m2_x4
 ADD = mybir.AluOpType.add
 
 P = 128
-PASSES = K // 512
-N_TILE = 512
-HALVES = N // N_TILE
+K_PASS = 512
+PASSES = K // K_PASS
+WORDS = K_PASS // 2
+N_HALF = 512
+HALVES = N // N_HALF
+W_HALF = N_HALF // P
 TILES = B // P
-RUN = 4
-HEAD = 6
-BLOCK = 4
-QUAD = 4
-PAIRS_FROM = 0
-SINGLES_FROM = 24
 BANKS = 8
-OUT_BUFS = 5
+
+RUN = 4
+SINGLES_FROM = TILES - 2 * RUN
+HALVES_FROM = TILES - RUN
+
+SPLIT_BUFS = 2 * RUN
+PAIR_BUFS = RUN
+RESULT_BUFS = 10
 
 
 def tile_groupfc_kernel(tc, data, W, b, out):
     nc = tc.nc
+    scalar_copy = nc.scalar.copy
+    vector_copy = nc.vector.tensor_copy
 
     with ExitStack() as ctx:
         keep = ctx.enter_context(tc.tile_pool(name="keep", bufs=1))
@@ -40,247 +46,219 @@ def tile_groupfc_kernel(tc, data, W, b, out):
 
         ident = keep.tile([P, P], F32, name="ident")
         make_identity(nc, ident[:])
+
         bias_row = keep.tile([P, N], BF16, name="bias_row")
         ones = keep.tile([P, P], BF16, name="ones")
         nc.vector.memset(bias_row[:].bitcast(U32), 0)
         nc.vector.memset(ones[:], 1.0)
         nc.scalar.dma_start(out=bias_row[0:1, :], in_=b.rearrange("(o n) -> o n", o=1))
 
+        data_rows = data.rearrange("(a p j) k -> a p j k", p=P, j=RUN)
+        out_rows = out.rearrange("(a p j) n -> a p j n", p=P, j=RUN)
         w_raw = {}
         x_raw = {}
-        data_rows = data.rearrange("(a p j) k -> a p j k", p=P, j=BLOCK)
-        out_rows = out.rearrange("(a p j) n -> a p j n", p=P, j=BLOCK)
 
         def load_w(first, count):
-            t = keep.tile([P, count, K], BF16, name="w_raw%d" % first)
-            nc.sync.dma_start(
-                out=t[:], in_=W[first * P:(first + count) * P, :].rearrange("(j p) k -> p j k", p=P))
+            raw = keep.tile([P, count, K], BF16, name="w_raw%d" % first)
+            rows = W[first * P:(first + count) * P, :]
+            nc.sync.dma_start(out=raw[:], in_=rows.rearrange("(j p) k -> p j k", p=P))
             for j in range(count):
-                w_raw[first + j] = t[:, j, :]
+                w_raw[first + j] = raw[:, j, :]
 
         def load_x(first, count):
-            block, j0 = divmod(first, BLOCK)
-            t = keep.tile([P, count, K], BF16, name="x_raw%d" % first)
-            nc.sync.dma_start(out=t[:], in_=data_rows[block][:, j0:j0 + count, :])
+            group, j0 = divmod(first, RUN)
+            raw = keep.tile([P, count, K], BF16, name="x_raw%d" % first)
+            nc.sync.dma_start(out=raw[:], in_=data_rows[group][:, j0:j0 + count, :])
             for j in range(count):
-                x_raw[first + j] = t[:, j, :]
+                x_raw[first + j] = raw[:, j, :]
 
         load_x(0, 1)
-        for r in range(4):
+        for r in range(W_HALF):
             load_w(r, 1)
         load_x(1, 1)
         load_x(2, 2)
-        load_w(4, 2)
-        load_w(6, 2)
-        load_x(4, 2)
-        runs = [(HEAD, HEAD + 2)] + [(first, first + RUN) for first in range(HEAD + 2, TILES, RUN)]
-        load_x(6, 2)
-        for first in range(8, TILES, RUN):
+        for r in range(W_HALF, 2 * W_HALF, 2):
+            load_w(r, 2)
+        for first in range(RUN, 2 * RUN, 2):
+            load_x(first, 2)
+        for first in range(2 * RUN, TILES, RUN):
             load_x(first, RUN)
 
         w_codes = keep.tile([P, PASSES, N], U32, name="w_codes", align_bytes=64)
         w_scales = keep.tile([P, PASSES, N], U8, name="w_scales", align_bytes=64)
         bias = keep.tile([P, N], F32, name="bias")
 
-        used = []
+        banks_taken = []
 
-        def t_bank():
-            used.append(0)
-            return psum.tile([P, PASSES, 2, P], F32, name="bank%d" % (len(used) % BANKS))
+        def next_bank(shape):
+            banks_taken.append(shape)
+            return psum.tile(shape, F32, name="bank%d" % (len(banks_taken) % BANKS))
 
-        def m_bank():
-            used.append(0)
-            return psum.tile([P, N_TILE], F32, name="bank%d" % (len(used) % BANKS))
+        def split(raw, index, copy):
+            words = stage.tile([P, PASSES, 2, P], F32, name="split%d" % (index % SPLIT_BUFS))
+            copy(out=words[:], in_=raw.bitcast(F32).rearrange("p (g q u) -> p g u q", g=PASSES, u=2))
+            return words
 
-        def copy_out(engine, dst, src):
-            if engine == "scalar":
-                nc.scalar.copy(out=dst, in_=src)
-            else:
-                nc.vector.tensor_copy(out=dst, in_=src)
-
-        def transpose_strided(raw, dst, engine):
-            words = raw.bitcast(F32)
-            bank = t_bank()
+        def transpose(raw, split_words, dst, copy):
+            bank = next_bank([P, PASSES, 2, P])
             for g in range(PASSES):
                 for u in range(2):
-                    nc.tensor.transpose(bank[:, g, u, :], words[:, 256 * g + u:256 * (g + 1):2], ident[:])
-            copy_out(engine, dst.bitcast(F32).rearrange("p (g r u) -> p g r u", g=PASSES, u=2),
-                     bank[:].rearrange("p g u r -> p g r u"))
+                    if split_words is None:
+                        src = raw.bitcast(F32)[:, WORDS * g + u:WORDS * (g + 1):2]
+                    else:
+                        src = split_words[:, g, u, :]
+                    nc.tensor.transpose(bank[:, g, u, :], src, ident[:])
+            copy(out=dst.bitcast(F32).rearrange("p (g r u) -> p g r u", g=PASSES, u=2),
+                 in_=bank[:].rearrange("p g u r -> p g r u"))
 
-        def transpose_split(split, dst, engine):
-            bank = t_bank()
-            for g in range(PASSES):
-                for u in range(2):
-                    nc.tensor.transpose(bank[:, g, u, :], split[:, g, u, :], ident[:])
-            copy_out(engine, dst.bitcast(F32).rearrange("p (g r u) -> p g r u", g=PASSES, u=2),
-                     bank[:].rearrange("p g u r -> p g r u"))
+        w_words = {}
+        w_turned = {}
 
-        w_grouped = {}
-        w_split_tiles = {}
+        def w_split(r, copy):
+            w_words[r] = split(w_raw[r], r, copy)
 
-        def w_transpose(r, engine):
-            t = stage.tile([P, K], BF16, name="w_grouped%d" % (r % 4), align_bytes=64)
-            if r in w_split_tiles:
-                transpose_split(w_split_tiles[r], t[:], engine)
-            else:
-                transpose_strided(w_raw[r], t[:], engine)
-            w_grouped[r] = t
-
-        def w_split(r, engine):
-            t = stage.tile([P, PASSES, 2, P], F32, name="split%d" % r)
-            copy_out(engine, t[:], w_raw[r].bitcast(F32).rearrange("p (g q u) -> p g u q", g=PASSES, u=2))
-            w_split_tiles[r] = t
+        def w_transpose(r, copy):
+            turned = stage.tile([P, K], BF16, name="w_turned%d" % (r % W_HALF), align_bytes=64)
+            transpose(w_raw[r], w_words.get(r), turned[:], copy)
+            w_turned[r] = turned
 
         def w_quantize(r):
             cols = slice(r * P, (r + 1) * P)
             for g in range(PASSES):
                 nc.vector.quantize_mx(
                     out=w_codes[:, g, cols].bitcast(E4M3X4), scales=w_scales[:, g, cols],
-                    in_=w_grouped[r][:, 512 * g:512 * (g + 1)])
+                    in_=w_turned[r][:, K_PASS * g:K_PASS * (g + 1)])
 
-        split = {}
-        grouped = {}
-        codes = {}
-        scales = {}
+        x_words = {}
+        x_turned = {}
+        x_codes = {}
+        x_scales = {}
         result = {}
 
-        def x_split(i, engine):
-            t = stage.tile([P, PASSES, 2, P], F32, name="split%d" % (i % 8))
-            copy_out(engine, t[:], x_raw[i].bitcast(F32).rearrange("p (g q u) -> p g u q", g=PASSES, u=2))
-            split[i] = t
+        def x_split(i, copy):
+            x_words[i] = split(x_raw[i], i, copy)
 
-        def x_transpose(i, engine):
-            q = i // 2
-            if i % 2 == 0:
-                grouped[q] = stage.tile([P, 2 * K], BF16, name="grouped%d" % (q % 4), align_bytes=64)
-            dst = grouped[q][:, (i % 2) * K:(i % 2 + 1) * K]
-            if i in split:
-                transpose_split(split[i], dst, engine)
-            else:
-                transpose_strided(x_raw[i], dst, engine)
+        def x_transpose(i):
+            pair, j = divmod(i, 2)
+            if j == 0:
+                x_turned[pair] = stage.tile(
+                    [P, 2 * K], BF16, name="x_turned%d" % (pair % PAIR_BUFS), align_bytes=64)
+            transpose(x_raw[i], x_words.get(i), x_turned[pair][:, j * K:(j + 1) * K], scalar_copy)
 
         def x_quantize(first, count):
-            q = first // 2
-            if first % 2 == 0:
-                codes[q] = stage.tile([P, 2 * PASSES * P], U32, name="codes%d" % (q % 4), align_bytes=64)
-                scales[q] = stage.tile([P, 2 * PASSES * P], U8, name="scales%d" % (q % 4), align_bytes=64)
-            j = first % 2
+            pair, j = divmod(first, 2)
+            if j == 0:
+                x_codes[pair] = stage.tile(
+                    [P, 2 * PASSES * P], U32, name="x_codes%d" % (pair % PAIR_BUFS), align_bytes=64)
+                x_scales[pair] = stage.tile(
+                    [P, 2 * PASSES * P], U8, name="x_scales%d" % (pair % PAIR_BUFS), align_bytes=64)
             cols = slice(j * PASSES * P, (j + count) * PASSES * P)
             nc.vector.quantize_mx(
-                out=codes[q][:, cols].bitcast(E5M2X4), scales=scales[q][:, cols],
-                in_=grouped[q][:, j * K:(j + count) * K])
+                out=x_codes[pair][:, cols].bitcast(E5M2X4), scales=x_scales[pair][:, cols],
+                in_=x_turned[pair][:, j * K:(j + count) * K])
+
+        def spread_bias(h):
+            n_cols = slice(h * N_HALF, (h + 1) * N_HALF)
+            spread = next_bank([P, N_HALF])
+            nc.tensor.matmul(spread[:], ones[:], bias_row[:, n_cols], start=True, stop=True)
+            scalar_copy(out=bias[:, n_cols], in_=spread[:])
 
         def multiply(i, h):
-            q, j = i // 2, i % 2
-            if i // QUAD not in result:
-                result[i // QUAD] = stage.tile([P, QUAD, N], F32, name="result%d" % (i // QUAD % OUT_BUFS))
-            n_cols = slice(h * N_TILE, (h + 1) * N_TILE)
-            acc = m_bank()
+            pair, j = divmod(i, 2)
+            if pair not in result:
+                result[pair] = stage.tile([P, 2, N], F32, name="result%d" % (pair % RESULT_BUFS))
+            n_cols = slice(h * N_HALF, (h + 1) * N_HALF)
+            acc = next_bank([P, N_HALF])
             for g in range(PASSES):
                 cols = slice((j * PASSES + g) * P, (j * PASSES + g + 1) * P)
                 nc.tensor.matmul_mx(
-                    out=acc[:], lhsT=codes[q][:, cols].bitcast(E5M2X4), lhsT_scale=scales[q][:, cols],
+                    out=acc[:],
+                    lhsT=x_codes[pair][:, cols].bitcast(E5M2X4), lhsT_scale=x_scales[pair][:, cols],
                     rhs=w_codes[:, g, n_cols].bitcast(E4M3X4), rhs_scale=w_scales[:, g, n_cols],
                     start=(g == 0), stop=(g == PASSES - 1))
-            nc.vector.tensor_tensor(out=result[i // QUAD][:, i % QUAD, n_cols], in0=acc[:], in1=bias[:, n_cols], op=ADD)
+            nc.vector.tensor_tensor(out=result[pair][:, j, n_cols], in0=acc[:], in1=bias[:, n_cols], op=ADD)
 
-        def store(i, count, n_cols):
-            block, j = divmod(i, BLOCK)
-            nc.sync.dma_start(out=out_rows[block][:, j:j + count, n_cols],
-                              in_=result[i // QUAD][:, i % QUAD:i % QUAD + count, n_cols])
+        def store(first, count, n_cols):
+            group, j0 = divmod(first, RUN)
+            pair, j = divmod(first, 2)
+            nc.sync.dma_start(out=out_rows[group][:, j0:j0 + count, n_cols],
+                              in_=result[pair][:, j:j + count, n_cols])
 
-        def spread_bias(h, engine):
-            n_cols = slice(h * N_TILE, (h + 1) * N_TILE)
-            spread = m_bank()
-            nc.tensor.matmul(spread[:], ones[:], bias_row[:, n_cols], start=True, stop=True)
-            copy_out(engine, bias[:, n_cols], spread[:])
-
-        def finish(i):
-            if i == TILES - 1:
-                store(i, 1, slice(N_TILE, N))
-            elif i >= SINGLES_FROM:
-                store(i, 1, slice(0, N))
-            elif i >= PAIRS_FROM:
-                if i % 2 == 1:
-                    store(i - 1, 2, slice(0, N))
-            elif i % QUAD == QUAD - 1:
-                store(i - QUAD + 1, QUAD, slice(0, N))
-
-        x_transpose(0, "scalar")
-        w_transpose(0, "scalar")
+        x_transpose(0)
+        w_transpose(0, scalar_copy)
         x_quantize(0, 1)
-        w_transpose(1, "scalar")
-        w_quantize(0)
-        w_transpose(2, "scalar")
-        w_quantize(1)
-        w_transpose(3, "vector")
-        w_quantize(2)
-        x_transpose(1, "scalar")
-        w_quantize(3)
-        spread_bias(0, "scalar")
+        for r in range(1, W_HALF):
+            w_transpose(r, vector_copy if r == W_HALF - 1 else scalar_copy)
+            w_quantize(r - 1)
+        x_transpose(1)
+        w_quantize(W_HALF - 1)
+        spread_bias(0)
         x_quantize(1, 1)
-        spread_bias(1, "scalar")
-        x_split(2, "vector")
-        x_split(3, "vector")
-        w_split(4, "scalar")
-        w_split(5, "scalar")
+        spread_bias(1)
+
+        x_split(2, vector_copy)
+        x_split(3, vector_copy)
+        w_split(W_HALF, scalar_copy)
+        w_split(W_HALF + 1, scalar_copy)
         multiply(0, 0)
-        w_split(6, "vector")
+        w_split(W_HALF + 2, vector_copy)
         multiply(1, 0)
-        w_split(7, "vector")
-        x_transpose(2, "scalar")
-        x_transpose(3, "scalar")
-        x_quantize(2, 1)
-        x_quantize(3, 1)
-        w_transpose(4, "scalar")
-        w_transpose(5, "vector")
-        w_transpose(6, "scalar")
-        w_transpose(7, "scalar")
-        w_quantize(4)
-        w_quantize(5)
-        w_quantize(6)
+        w_split(W_HALF + 3, vector_copy)
+
+        for i in (2, 3):
+            x_transpose(i)
+        for i in (2, 3):
+            x_quantize(i, 1)
+        for r in range(W_HALF, 2 * W_HALF):
+            w_transpose(r, vector_copy if r == W_HALF + 1 else scalar_copy)
+        for r in range(W_HALF, 2 * W_HALF - 1):
+            w_quantize(r)
         multiply(2, 0)
-        w_quantize(7)
+        w_quantize(2 * W_HALF - 1)
         multiply(3, 0)
-        x_split(8, "scalar")
-        x_split(9, "scalar")
-        for i in range(4, 8):
-            x_transpose(i, "scalar")
-        x_split(10, "vector")
-        x_split(11, "vector")
-        todo = [(i, 1) for i in range(4)] + [(i, h) for i in range(4, TILES) for h in range(HALVES)]
+
+        for i in range(RUN + 2, 2 * RUN):
+            x_split(i, scalar_copy)
+        for i in range(RUN, 2 * RUN):
+            x_transpose(i)
+        x_split(3 * RUN - 1, scalar_copy)
+        for i in range(2 * RUN, 3 * RUN - 1):
+            x_split(i, vector_copy)
+
+        todo = [(i, 1) for i in range(RUN)] + [(i, h) for i in range(RUN, TILES) for h in range(HALVES)]
 
         def advance(count):
-            for i, h in todo[:count]:
-                multiply(i, h)
-                if i == TILES - 1 and h == 0:
-                    store(i, 1, slice(0, N_TILE))
-                if h == 1:
-                    finish(i)
             for step in range(count):
-                todo.pop(0)
+                i, h = todo.pop(0)
+                multiply(i, h)
+                if i >= HALVES_FROM:
+                    store(i, 1, slice(h * N_HALF, (h + 1) * N_HALF))
+                elif h == 1 and i >= SINGLES_FROM:
+                    store(i, 1, slice(0, N))
+                elif h == 1 and i % 2 == 1:
+                    store(i - 1, 2, slice(0, N))
 
-        advance(2)
-        x_quantize(4, 2)
-        advance(2)
-        x_quantize(6, 2)
+        for first in range(RUN, 2 * RUN, 2):
+            advance(HALVES)
+            x_quantize(first, 2)
 
-        for first in range(8, TILES - RUN, RUN):
-            last = first + RUN
-            for i in range(first, last):
-                x_transpose(i, "scalar")
-            for i in range(last, last + RUN):
-                x_split(i, "scalar")
-            for pair in range(first, last, 2):
-                advance(4)
-                x_quantize(pair, 2)
-        for i in range(TILES - 4, TILES - 2):
-            x_transpose(i, "scalar")
-        advance(4)
-        x_quantize(TILES - 4, 2)
-        advance(4)
-        for i in range(TILES - 2, TILES):
-            x_transpose(i, "scalar")
+        for first in range(2 * RUN, TILES - RUN, RUN):
+            for i in range(first, first + RUN):
+                x_transpose(i)
+            for i in range(first + RUN, first + 2 * RUN):
+                x_split(i, scalar_copy)
+            for pair_first in range(first, first + RUN, 2):
+                advance(2 * HALVES)
+                x_quantize(pair_first, 2)
+
+        last_pairs = (TILES - RUN, TILES - 2)
+        for i in range(last_pairs[0], last_pairs[1]):
+            x_transpose(i)
+        advance(2 * HALVES)
+        x_quantize(last_pairs[0], 2)
+        advance(2 * HALVES)
+        for i in range(last_pairs[1], TILES):
+            x_transpose(i)
         advance(1)
-        x_quantize(TILES - 2, 2)
+        x_quantize(last_pairs[1], 2)
         advance(len(todo))

from contextlib import ExitStack

import concourse.mybir as mybir
from concourse.masks import make_identity

B, K, N = 4096, 1024, 1024
FLOPS = 2 * B * K * N

F32 = mybir.dt.float32
BF16 = mybir.dt.bfloat16
U32 = mybir.dt.uint32
U8 = mybir.dt.uint8
E4M3X4 = mybir.dt.float8_e4m3fn_x4
E5M2X4 = mybir.dt.float8_e5m2_x4
ADD = mybir.AluOpType.add

P = 128
K_PASS = 512
PASSES = K // K_PASS
WORDS = K_PASS // 2
N_HALF = 512
HALVES = N // N_HALF
W_HALF = N_HALF // P
TILES = B // P
BANKS = 8

RUN = 4
SINGLES_FROM = TILES - 2 * RUN
HALVES_FROM = TILES - RUN

SPLIT_BUFS = 2 * RUN
PAIR_BUFS = RUN
RESULT_BUFS = 10


def tile_groupfc_kernel(tc, data, W, b, out):
    nc = tc.nc
    scalar_copy = nc.scalar.copy
    vector_copy = nc.vector.tensor_copy

    with ExitStack() as ctx:
        keep = ctx.enter_context(tc.tile_pool(name="keep", bufs=1))
        stage = ctx.enter_context(tc.tile_pool(name="stage", bufs=1))
        psum = ctx.enter_context(tc.psum_pool(name="psum", bufs=1))
        ctx.enter_context(tc.manual_schedule())

        ident = keep.tile([P, P], F32, name="ident")
        make_identity(nc, ident[:])

        bias_row = keep.tile([P, N], BF16, name="bias_row")
        ones = keep.tile([P, P], BF16, name="ones")
        nc.vector.memset(bias_row[:].bitcast(U32), 0)
        nc.vector.memset(ones[:], 1.0)
        nc.scalar.dma_start(out=bias_row[0:1, :], in_=b.rearrange("(o n) -> o n", o=1))

        data_rows = data.rearrange("(a p j) k -> a p j k", p=P, j=RUN)
        out_rows = out.rearrange("(a p j) n -> a p j n", p=P, j=RUN)
        w_raw = {}
        x_raw = {}

        def load_w(first, count):
            raw = keep.tile([P, count, K], BF16, name="w_raw%d" % first)
            rows = W[first * P:(first + count) * P, :]
            nc.sync.dma_start(out=raw[:], in_=rows.rearrange("(j p) k -> p j k", p=P))
            for j in range(count):
                w_raw[first + j] = raw[:, j, :]

        def load_x(first, count):
            group, j0 = divmod(first, RUN)
            raw = keep.tile([P, count, K], BF16, name="x_raw%d" % first)
            nc.sync.dma_start(out=raw[:], in_=data_rows[group][:, j0:j0 + count, :])
            for j in range(count):
                x_raw[first + j] = raw[:, j, :]

        load_x(0, 1)
        for r in range(W_HALF):
            load_w(r, 1)
        load_x(1, 1)
        load_x(2, 2)
        for r in range(W_HALF, 2 * W_HALF, 2):
            load_w(r, 2)
        for first in range(RUN, 2 * RUN, 2):
            load_x(first, 2)
        for first in range(2 * RUN, TILES, RUN):
            load_x(first, RUN)

        w_codes = keep.tile([P, PASSES, N], U32, name="w_codes", align_bytes=64)
        w_scales = keep.tile([P, PASSES, N], U8, name="w_scales", align_bytes=64)
        bias = keep.tile([P, N], F32, name="bias")

        banks_taken = []

        def next_bank(shape):
            banks_taken.append(shape)
            return psum.tile(shape, F32, name="bank%d" % (len(banks_taken) % BANKS))

        def split(raw, index, copy):
            words = stage.tile([P, PASSES, 2, P], F32, name="split%d" % (index % SPLIT_BUFS))
            copy(out=words[:], in_=raw.bitcast(F32).rearrange("p (g q u) -> p g u q", g=PASSES, u=2))
            return words

        def transpose(raw, split_words, dst, copy):
            bank = next_bank([P, PASSES, 2, P])
            for g in range(PASSES):
                for u in range(2):
                    if split_words is None:
                        src = raw.bitcast(F32)[:, WORDS * g + u:WORDS * (g + 1):2]
                    else:
                        src = split_words[:, g, u, :]
                    nc.tensor.transpose(bank[:, g, u, :], src, ident[:])
            copy(out=dst.bitcast(F32).rearrange("p (g r u) -> p g r u", g=PASSES, u=2),
                 in_=bank[:].rearrange("p g u r -> p g r u"))

        w_words = {}
        w_turned = {}

        def w_split(r, copy):
            w_words[r] = split(w_raw[r], r, copy)

        def w_transpose(r, copy):
            turned = stage.tile([P, K], BF16, name="w_turned%d" % (r % W_HALF), align_bytes=64)
            transpose(w_raw[r], w_words.get(r), turned[:], copy)
            w_turned[r] = turned

        def w_quantize(r):
            cols = slice(r * P, (r + 1) * P)
            for g in range(PASSES):
                nc.vector.quantize_mx(
                    out=w_codes[:, g, cols].bitcast(E4M3X4), scales=w_scales[:, g, cols],
                    in_=w_turned[r][:, K_PASS * g:K_PASS * (g + 1)])

        x_words = {}
        x_turned = {}
        x_codes = {}
        x_scales = {}
        result = {}

        def x_split(i, copy):
            x_words[i] = split(x_raw[i], i, copy)

        def x_transpose(i):
            pair, j = divmod(i, 2)
            if j == 0:
                x_turned[pair] = stage.tile(
                    [P, 2 * K], BF16, name="x_turned%d" % (pair % PAIR_BUFS), align_bytes=64)
            transpose(x_raw[i], x_words.get(i), x_turned[pair][:, j * K:(j + 1) * K], scalar_copy)

        def x_quantize(first, count):
            pair, j = divmod(first, 2)
            if j == 0:
                x_codes[pair] = stage.tile(
                    [P, 2 * PASSES * P], U32, name="x_codes%d" % (pair % PAIR_BUFS), align_bytes=64)
                x_scales[pair] = stage.tile(
                    [P, 2 * PASSES * P], U8, name="x_scales%d" % (pair % PAIR_BUFS), align_bytes=64)
            cols = slice(j * PASSES * P, (j + count) * PASSES * P)
            nc.vector.quantize_mx(
                out=x_codes[pair][:, cols].bitcast(E5M2X4), scales=x_scales[pair][:, cols],
                in_=x_turned[pair][:, j * K:(j + count) * K])

        def spread_bias(h):
            n_cols = slice(h * N_HALF, (h + 1) * N_HALF)
            spread = next_bank([P, N_HALF])
            nc.tensor.matmul(spread[:], ones[:], bias_row[:, n_cols], start=True, stop=True)
            scalar_copy(out=bias[:, n_cols], in_=spread[:])

        def multiply(i, h):
            pair, j = divmod(i, 2)
            if pair not in result:
                result[pair] = stage.tile([P, 2, N], F32, name="result%d" % (pair % RESULT_BUFS))
            n_cols = slice(h * N_HALF, (h + 1) * N_HALF)
            acc = next_bank([P, N_HALF])
            for g in range(PASSES):
                cols = slice((j * PASSES + g) * P, (j * PASSES + g + 1) * P)
                nc.tensor.matmul_mx(
                    out=acc[:],
                    lhsT=x_codes[pair][:, cols].bitcast(E5M2X4), lhsT_scale=x_scales[pair][:, cols],
                    rhs=w_codes[:, g, n_cols].bitcast(E4M3X4), rhs_scale=w_scales[:, g, n_cols],
                    start=(g == 0), stop=(g == PASSES - 1))
            nc.vector.tensor_tensor(out=result[pair][:, j, n_cols], in0=acc[:], in1=bias[:, n_cols], op=ADD)

        def store(first, count, n_cols):
            group, j0 = divmod(first, RUN)
            pair, j = divmod(first, 2)
            nc.sync.dma_start(out=out_rows[group][:, j0:j0 + count, n_cols],
                              in_=result[pair][:, j:j + count, n_cols])

        x_transpose(0)
        w_transpose(0, scalar_copy)
        x_quantize(0, 1)
        for r in range(1, W_HALF):
            w_transpose(r, vector_copy if r == W_HALF - 1 else scalar_copy)
            w_quantize(r - 1)
        x_transpose(1)
        w_quantize(W_HALF - 1)
        spread_bias(0)
        x_quantize(1, 1)
        spread_bias(1)

        x_split(2, vector_copy)
        x_split(3, vector_copy)
        w_split(W_HALF, scalar_copy)
        w_split(W_HALF + 1, scalar_copy)
        multiply(0, 0)
        w_split(W_HALF + 2, vector_copy)
        multiply(1, 0)
        w_split(W_HALF + 3, vector_copy)

        for i in (2, 3):
            x_transpose(i)
        for i in (2, 3):
            x_quantize(i, 1)
        for r in range(W_HALF, 2 * W_HALF):
            w_transpose(r, vector_copy if r == W_HALF + 1 else scalar_copy)
        for r in range(W_HALF, 2 * W_HALF - 1):
            w_quantize(r)
        multiply(2, 0)
        w_quantize(2 * W_HALF - 1)
        multiply(3, 0)

        for i in range(RUN + 2, 2 * RUN):
            x_split(i, scalar_copy)
        for i in range(RUN, 2 * RUN):
            x_transpose(i)
        x_split(3 * RUN - 1, scalar_copy)
        for i in range(2 * RUN, 3 * RUN - 1):
            x_split(i, vector_copy)

        todo = [(i, 1) for i in range(RUN)] + [(i, h) for i in range(RUN, TILES) for h in range(HALVES)]

        def advance(count):
            for step in range(count):
                i, h = todo.pop(0)
                multiply(i, h)
                if i >= HALVES_FROM:
                    store(i, 1, slice(h * N_HALF, (h + 1) * N_HALF))
                elif h == 1 and i >= SINGLES_FROM:
                    store(i, 1, slice(0, N))
                elif h == 1 and i % 2 == 1:
                    store(i - 1, 2, slice(0, N))

        for first in range(RUN, 2 * RUN, 2):
            advance(HALVES)
            x_quantize(first, 2)

        for first in range(2 * RUN, TILES - RUN, RUN):
            for i in range(first, first + RUN):
                x_transpose(i)
            for i in range(first + RUN, first + 2 * RUN):
                x_split(i, scalar_copy)
            for pair_first in range(first, first + RUN, 2):
                advance(2 * HALVES)
                x_quantize(pair_first, 2)

        last_pairs = (TILES - RUN, TILES - 2)
        for i in range(last_pairs[0], last_pairs[1]):
            x_transpose(i)
        advance(2 * HALVES)
        x_quantize(last_pairs[0], 2)
        advance(2 * HALVES)
        for i in range(last_pairs[1], TILES):
            x_transpose(i)
        advance(1)
        x_quantize(last_pairs[1], 2)
        advance(len(todo))
